import numpy as np
import ml_dtypes


def mxq(x, axis, fmt="e4m3"):
    dtype, down = {"e4m3": (ml_dtypes.float8_e4m3fn, 7), "e5m2": (ml_dtypes.float8_e5m2, 14)}[fmt]
    v = np.moveaxis(np.asarray(x, np.float32).astype(ml_dtypes.bfloat16).astype(np.float64), axis, -1)
    blocks = v.reshape(v.shape[:-1] + (-1, 32))
    amax = np.abs(blocks).max(-1, keepdims=True)
    byte = np.maximum(np.where(amax > 0, np.frexp(amax)[1] - 1 + 127, 0) - down, 1)
    scale = np.exp2(byte - 127.0)
    codes = (blocks / scale).astype(np.float32).astype(dtype).astype(np.float64)
    return np.moveaxis((codes * scale).reshape(v.shape), -1, axis)


WIDE = False


def mx_kscale(k):
    if not WIDE:
        return np.ones(k)
    levels = np.array([10, -10, 5, -5, 0])
    a = np.random.permutation(np.resize(levels, k // 512 * 4)).reshape(k // 512, 4)
    idx = np.arange(k)
    return np.exp2(a[idx // 512, idx % 128 // 32])


BF16 = ml_dtypes.bfloat16


def bf(x):
    return np.asarray(x, np.float32).astype(BF16)


def f64(x):
    return np.asarray(x).astype(np.float64)


B, H, T, N, D, GRID = 1, 4, 512, 2048, 256, 32


def rot_pairs(v):
    return np.stack((-v[..., 1::2], v[..., ::2]), axis=-1).reshape(v.shape)


def rope(v, c, s):
    return v * c + rot_pairs(v) * s


def setup_inputs():
    s = np.repeat(mx_kscale(N)[::2], 2)
    t = mx_kscale(T)
    u = np.random.random((T, N))
    return {"Q": bf(np.random.standard_normal((B, H, T, N)) * s),
            "K": bf(np.random.standard_normal((B, H, T, N)) * t[:, None] / s),
            "V": bf(np.random.standard_normal((B, 1, T, D)) * 2.0 / np.sqrt(T) / t[:, None]),
            "cos_t": bf(np.cos(2.0 * np.pi * u)),
            "sin_t": bf(np.sin(2.0 * np.pi * u))}


def reference(Q, K, V, cos_t, sin_t):
    c, s = f64(cos_t), f64(sin_t)
    qr = rope(f64(Q), c, s)
    kr = rope(f64(K), c, s)
    scores = (mxq(qr, 3, "e4m3") @ mxq(kr, 3, "e4m3").transpose(0, 1, 3, 2)) / np.sqrt(N)
    return mxq(scores, 3, "e4m3") @ mxq(f64(V), 2, "e4m3")

@@ -1,0 +1,196 @@
+from contextlib import ExitStack
+
+import concourse.mybir as mybir
+from concourse.masks import make_identity
+
+F32 = mybir.dt.float32
+BF16 = mybir.dt.bfloat16
+U32 = mybir.dt.uint32
+U8 = mybir.dt.uint8
+FP8X4 = mybir.dt.float8_e4m3fn_x4
+MULT = mybir.AluOpType.mult
+COPY = mybir.ActivationFunctionType.Copy
+
+P = 128
+H = 4
+T = 512
+N = 2048
+D = 256
+TT = T // P
+NG = N // 512
+FLOPS = 2 * H * T * T * N + 2 * H * T * T * D
+
+
+def tile_bidirectionalattention_pa_kernel(tc, Q, K, V, cos_t, sin_t, out):
+    nc = tc.nc
+    Qf = Q.flatten_outer_dims()
+    Kf = K.flatten_outer_dims()
+    Vf = V.flatten_outer_dims()
+    outf = out.flatten_outer_dims()
+    inv_sqrt_n = 1.0 / (float(N) ** 0.5)
+
+    with ExitStack() as ctx:
+        const = ctx.enter_context(tc.tile_pool(name="const", bufs=1))
+        xpool = ctx.enter_context(tc.tile_pool(name="xpool", bufs=4))
+        prod = ctx.enter_context(tc.tile_pool(name="prod", bufs=2))
+        gpool = ctx.enter_context(tc.tile_pool(name="gpool", bufs=3))
+        qpool = ctx.enter_context(tc.tile_pool(name="qpool", bufs=3))
+        spool = ctx.enter_context(tc.tile_pool(name="spool", bufs=2))
+        accp = ctx.enter_context(tc.psum_pool(name="accp", bufs=4))
+        scp = ctx.enter_context(tc.psum_pool(name="scp", bufs=2))
+        op = ctx.enter_context(tc.psum_pool(name="op", bufs=2))
+
+        ident = const.tile([P, P], F32, name="ident")
+        make_identity(nc, ident[:])
+
+        cos_sb = []
+        sin_sb = []
+        for tau in range(TT):
+            cos_sb.append(const.tile([P, N], BF16, name="cos%d" % tau))
+            sin_sb.append(const.tile([P, N], BF16, name="sin%d" % tau))
+        kcodes = const.tile([P, H * TT, 512], U32, name="kcodes", align_bytes=64)
+        kscales = const.tile([P, H * TT, 512], U8, name="kscales", align_bytes=64)
+        v_raw = const.tile([P, 4, D], BF16, name="v_raw")
+        v_grp = const.tile([P, D, 4], BF16, name="v_grp", align_bytes=64)
+        vcodes = const.tile([P, D], U32, name="vcodes", align_bytes=64)
+        vscales = const.tile([P, D], U8, name="vscales", align_bytes=64)
+
+        units = []
+        for which in range(2):
+            for tau in range(TT):
+                for h in range(H):
+                    units.append((which, tau, h))
+        NU = len(units)
+        state = {}
+
+        def load_tables(tau):
+            rows = slice(tau * P, (tau + 1) * P)
+            nc.sync.dma_start(out=cos_sb[tau][:], in_=cos_t[rows, :])
+            nc.sync.dma_start(out=sin_sb[tau][:], in_=sin_t[rows, :])
+
+        def load(u):
+            which, tau, h = units[u]
+            src = Kf if which == 0 else Qf
+            x = xpool.tile([P, N], BF16, name="x")
+            r0 = h * T + tau * P
+            nc.sync.dma_start(out=x[:], in_=src[r0 : r0 + P, :])
+            state[("x", u)] = x
+
+        def products(u):
+            which, tau, h = units[u]
+            x = state[("x", u)]
+            xv = x[:].rearrange("p (i e) -> p e i", e=2)
+            cv = cos_sb[tau][:].rearrange("p (i e) -> p e i", e=2)
+            sv = sin_sb[tau][:].rearrange("p (i e) -> p e i", e=2)
+            a = prod.tile([P, 2, N // 2], F32, name="a")
+            b = prod.tile([P, 2, N // 2], F32, name="b")
+            nc.vector.tensor_tensor(out=a[:], in0=xv, in1=cv, op=MULT)
+            nc.vector.scalar_tensor_tensor(
+                out=b[:, 0, :], in0=xv[:, 1, :], scalar=-1.0, in1=sv[:, 0, :], op0=MULT, op1=MULT
+            )
+            nc.vector.tensor_tensor(out=b[:, 1, :], in0=xv[:, 0, :], in1=sv[:, 1, :], op=MULT)
+            state[("ab", u)] = (a, b)
+
+        def rotate_sum(u):
+            a, b = state[("ab", u)]
+            grp = gpool.tile([P, NG, P, 4], BF16, name="grp", align_bytes=64)
+            for g in range(NG):
+                ps = accp.tile([P, 4, P], F32, name="ps")
+                for half in range(2):
+                    for e in range(2):
+                        c = 2 * g + half
+                        cols = slice(c * P, (c + 1) * P)
+                        dst = ps[:, 2 * half + e, :]
+                        nc.tensor.matmul(
+                            out=dst, lhsT=a[:, e, cols], rhs=ident[:], start=True, stop=False, is_transpose=True
+                        )
+                        nc.tensor.matmul(
+                            out=dst, lhsT=b[:, e, cols], rhs=ident[:], start=False, stop=True, is_transpose=True
+                        )
+                nc.scalar.copy(out=grp[:, g, :, :], in_=ps[:].rearrange("p j t -> p t j"))
+            state[("grp", u)] = grp
+
+        def quantise(u):
+            which, tau, h = units[u]
+            grp = state[("grp", u)]
+            if which == 0:
+                codes = kcodes[:, h * TT + tau, :]
+                scales = kscales[:, h * TT + tau, :]
+            else:
+                qc = qpool.tile([P, 512], U32, name="qc", align_bytes=64)
+                qs = qpool.tile([P, 512], U8, name="qs", align_bytes=64)
+                codes = qc[:]
+                scales = qs[:]
+                state[("q", u)] = (qc, qs)
+            nc.vector.quantize_mx(
+                out=codes.bitcast(FP8X4), scales=scales, in_=grp[:].rearrange("p g t j -> p (g t j)")
+            )
+
+        def scores(u):
+            which, tau, h = units[u]
+            if which == 0:
+                return
+            qc, qs = state[("q", u)]
+            sc = scp.tile([P, TT, P], F32, name="sc")
+            for tk in range(TT):
+                for g in range(NG):
+                    cols = slice(g * P, (g + 1) * P)
+                    nc.tensor.matmul_mx(
+                        out=sc[:, tk, :],
+                        lhsT=kcodes[:, h * TT + tk, cols].bitcast(FP8X4),
+                        lhsT_scale=kscales[:, h * TT + tk, cols],
+                        rhs=qc[:, cols].bitcast(FP8X4),
+                        rhs_scale=qs[:, cols],
+                        start=(g == 0),
+                        stop=(g == NG - 1),
+                    )
+            sg = spool.tile([P, P, 4], BF16, name="sg", align_bytes=64)
+            nc.scalar.activation(out=sg[:], in_=sc[:].rearrange("p j q -> p q j"), func=COPY, scale=inv_sqrt_n)
+            state[("sg", u)] = sg
+
+        def output(u):
+            which, tau, h = units[u]
+            if which == 0:
+                return
+            sg = state[("sg", u)]
+            scd = spool.tile([P, P], U32, name="scd", align_bytes=64)
+            ssc = spool.tile([P, P], U8, name="ssc", align_bytes=64)
+            nc.vector.quantize_mx(out=scd[:].bitcast(FP8X4), scales=ssc[:], in_=sg[:].rearrange("p q j -> p (q j)"))
+            o_ps = op.tile([P, D], F32, name="o_ps")
+            nc.tensor.matmul_mx(
+                out=o_ps[:],
+                lhsT=scd[:].bitcast(FP8X4),
+                lhsT_scale=ssc[:],
+                rhs=vcodes[:].bitcast(FP8X4),
+                rhs_scale=vscales[:],
+                start=True,
+                stop=True,
+            )
+            o_sb = spool.tile([P, D], F32, name="o_sb")
+            nc.scalar.copy(out=o_sb[:], in_=o_ps[:])
+            r0 = h * T + tau * P
+            nc.sync.dma_start(out=outf[r0 : r0 + P, :], in_=o_sb[:])
+
+        load_tables(0)
+        load(0)
+        load(1)
+        nc.scalar.dma_start(out=v_raw[:], in_=Vf.rearrange("(j p) d -> p j d", p=P))
+        nc.scalar.copy(out=v_grp[:], in_=v_raw[:].rearrange("p j d -> p d j"))
+        nc.vector.quantize_mx(
+            out=vcodes[:].bitcast(FP8X4), scales=vscales[:], in_=v_grp[:].rearrange("p d j -> p (d j)")
+        )
+
+        for s in range(NU + 2):
+            if s + 2 < NU:
+                which, tau, h = units[s + 2]
+                if which == 0 and h == 0 and tau > 0:
+                    load_tables(tau)
+                load(s + 2)
+            if s < NU:
+                products(s)
+                rotate_sum(s)
+            if 0 <= s - 1 < NU:
+                quantise(s - 1)
+                scores(s - 1)
+            if 0 <= s - 2 < NU:
+                output(s - 2)

@@ -18,6 +18,11 @@ N = 2048
 D = 256
 TT = T // P
 NG = N // 512
+NI = N // 2
+NB = 384
+NBB = NB // P
+NTB = 8 + NBB
+AHEAD = 3
 FLOPS = 2 * H * T * T * N + 2 * H * T * T * D
 
 
@@ -31,23 +36,29 @@ def tile_bidirectionalattention_pa_kernel(tc, Q, K, V, cos_t, sin_t, out):
 
     with ExitStack() as ctx:
         const = ctx.enter_context(tc.tile_pool(name="const", bufs=1))
-        xpool = ctx.enter_context(tc.tile_pool(name="xpool", bufs=4))
-        prod = ctx.enter_context(tc.tile_pool(name="prod", bufs=2))
+        xpool = ctx.enter_context(tc.tile_pool(name="xpool", bufs=AHEAD + 1))
+        prod = ctx.enter_context(tc.tile_pool(name="prod", bufs=3))
         gpool = ctx.enter_context(tc.tile_pool(name="gpool", bufs=3))
-        qpool = ctx.enter_context(tc.tile_pool(name="qpool", bufs=3))
+        qpool = ctx.enter_context(tc.tile_pool(name="qpool", bufs=2))
         spool = ctx.enter_context(tc.tile_pool(name="spool", bufs=2))
-        accp = ctx.enter_context(tc.psum_pool(name="accp", bufs=4))
-        scp = ctx.enter_context(tc.psum_pool(name="scp", bufs=2))
-        op = ctx.enter_context(tc.psum_pool(name="op", bufs=2))
+        tabp = ctx.enter_context(tc.psum_pool(name="tabp", bufs=1))
+        accp = ctx.enter_context(tc.psum_pool(name="accp", bufs=3))
+        scp = ctx.enter_context(tc.psum_pool(name="scp", bufs=1))
+        op = ctx.enter_context(tc.psum_pool(name="op", bufs=1))
+        ctx.enter_context(tc.manual_schedule())
 
         ident = const.tile([P, P], F32, name="ident")
         make_identity(nc, ident[:])
 
         cos_sb = []
         sin_sb = []
+        sneg = []
+        tab_t = []
         for tau in range(TT):
             cos_sb.append(const.tile([P, N], BF16, name="cos%d" % tau))
             sin_sb.append(const.tile([P, N], BF16, name="sin%d" % tau))
+            sneg.append(const.tile([P, NI - NB], BF16, name="sneg%d" % tau))
+            tab_t.append(const.tile([P, NTB, P], F32, name="tabt%d" % tau))
         kcodes = const.tile([P, H * TT, 512], U32, name="kcodes", align_bytes=64)
         kscales = const.tile([P, H * TT, 512], U8, name="kscales", align_bytes=64)
         v_raw = const.tile([P, 4, D], BF16, name="v_raw")
@@ -76,20 +87,75 @@ def tile_bidirectionalattention_pa_kernel(tc, Q, K, V, cos_t, sin_t, out):
             nc.sync.dma_start(out=x[:], in_=src[r0 : r0 + P, :])
             state[("x", u)] = x
 
-        def products(u):
-            which, tau, h = units[u]
-            x = state[("x", u)]
-            xv = x[:].rearrange("p (i e) -> p e i", e=2)
-            cv = cos_sb[tau][:].rearrange("p (i e) -> p e i", e=2)
+        def negate_sin(tau):
             sv = sin_sb[tau][:].rearrange("p (i e) -> p e i", e=2)
-            a = prod.tile([P, 2, N // 2], F32, name="a")
-            b = prod.tile([P, 2, N // 2], F32, name="b")
-            nc.vector.tensor_tensor(out=a[:], in0=xv, in1=cv, op=MULT)
-            nc.vector.scalar_tensor_tensor(
-                out=b[:, 0, :], in0=xv[:, 1, :], scalar=-1.0, in1=sv[:, 0, :], op0=MULT, op1=MULT
-            )
-            nc.vector.tensor_tensor(out=b[:, 1, :], in0=xv[:, 0, :], in1=sv[:, 1, :], op=MULT)
+            nc.scalar.mul(out=sneg[tau][:], in_=sv[:, 0, NB:NI], mul=-1.0)
+
+        def tables_flip(tau):
+            cw = cos_sb[tau][:].bitcast(F32)
+            sw = sin_sb[tau][:].bitcast(F32)
+            for b0 in range(0, NTB, 4):
+                n = min(4, NTB - b0)
+                ps = accp.tile([P, 4, P], F32, name="ps")
+                for k in range(n):
+                    b = b0 + k
+                    srcw = cw[:, b * P : (b + 1) * P] if b < 8 else sw[:, (b - 8) * P : (b - 7) * P]
+                    nc.tensor.transpose(ps[:, k, :], srcw, ident[:])
+                nc.scalar.copy(out=tab_t[tau][:, b0 : b0 + n, :], in_=ps[:, 0:n, :])
+
+        def tables_back(tau, part):
+            if part == 0:
+                t = tabp.tile([P, 512], F32, name="tabc0")
+                blocks = range(0, 4)
+            elif part == 1:
+                t = tabp.tile([P, 512], F32, name="tabc1")
+                blocks = range(4, 8)
+            else:
+                t = tabp.tile([P, 512], F32, name="tabs")
+                blocks = range(8, NTB)
+            for k, b in enumerate(blocks):
+                nc.tensor.transpose(t[:, k * P : (k + 1) * P], tab_t[tau][:, b, :], ident[:])
+            state[("tab", part)] = t
+
+        def pair_view(ap):
+            return ap.rearrange("p (i e) -> p e i", e=2)
+
+        def products_begin(u):
+            a = prod.tile([P, 2, NI], F32, name="a")
+            b = prod.tile([P, 2, NI], F32, name="b")
             state[("ab", u)] = (a, b)
+
+        def product_cos(u, part):
+            which, tau, h = units[u]
+            xv = pair_view(state[("x", u)][:])
+            a, b = state[("ab", u)]
+            rng = slice(part * 512, (part + 1) * 512)
+            if u == 0:
+                cv = pair_view(cos_sb[tau][:])[:, :, rng]
+            else:
+                cv = pair_view(state[("tab", part)][:].bitcast(BF16))
+            nc.vector.tensor_tensor(out=a[:, :, rng], in0=xv[:, :, rng], in1=cv, op=MULT)
+
+        def product_sin_vector(u):
+            which, tau, h = units[u]
+            xv = pair_view(state[("x", u)][:])
+            a, b = state[("ab", u)]
+            if u == 0:
+                sv = pair_view(sin_sb[tau][:])[:, :, 0:NB]
+            else:
+                sv = pair_view(state[("tab", 2)][:].bitcast(BF16)[:, 0 : 2 * NB])
+            nc.vector.scalar_tensor_tensor(
+                out=b[:, 0, 0:NB], in0=xv[:, 1, 0:NB], scalar=-1.0, in1=sv[:, 0, :], op0=MULT, op1=MULT
+            )
+            nc.vector.tensor_tensor(out=b[:, 1, 0:NB], in0=xv[:, 0, 0:NB], in1=sv[:, 1, :], op=MULT)
+
+        def product_sin_gpsimd(u):
+            which, tau, h = units[u]
+            xv = pair_view(state[("x", u)][:])
+            sv = pair_view(sin_sb[tau][:])
+            a, b = state[("ab", u)]
+            nc.gpsimd.tensor_tensor(out=b[:, 0, NB:NI], in0=xv[:, 1, NB:NI], in1=sneg[tau][:], op=MULT)
+            nc.gpsimd.tensor_tensor(out=b[:, 1, NB:NI], in0=xv[:, 0, NB:NI], in1=sv[:, 1, NB:NI], op=MULT)
 
         def rotate_sum(u):
             a, b = state[("ab", u)]
@@ -128,8 +194,6 @@ def tile_bidirectionalattention_pa_kernel(tc, Q, K, V, cos_t, sin_t, out):
 
         def scores(u):
             which, tau, h = units[u]
-            if which == 0:
-                return
             qc, qs = state[("q", u)]
             sc = scp.tile([P, TT, P], F32, name="sc")
             for tk in range(TT):
@@ -144,18 +208,23 @@ def tile_bidirectionalattention_pa_kernel(tc, Q, K, V, cos_t, sin_t, out):
                         start=(g == 0),
                         stop=(g == NG - 1),
                     )
+            state[("sc", u)] = sc
+
+        def scores_out(u):
+            sc = state[("sc", u)]
             sg = spool.tile([P, P, 4], BF16, name="sg", align_bytes=64)
             nc.scalar.activation(out=sg[:], in_=sc[:].rearrange("p j q -> p q j"), func=COPY, scale=inv_sqrt_n)
             state[("sg", u)] = sg
 
-        def output(u):
-            which, tau, h = units[u]
-            if which == 0:
-                return
+        def scores_quantise(u):
             sg = state[("sg", u)]
             scd = spool.tile([P, P], U32, name="scd", align_bytes=64)
             ssc = spool.tile([P, P], U8, name="ssc", align_bytes=64)
             nc.vector.quantize_mx(out=scd[:].bitcast(FP8X4), scales=ssc[:], in_=sg[:].rearrange("p q j -> p (q j)"))
+            state[("scd", u)] = (scd, ssc)
+
+        def values(u):
+            scd, ssc = state[("scd", u)]
             o_ps = op.tile([P, D], F32, name="o_ps")
             nc.tensor.matmul_mx(
                 out=o_ps[:],
@@ -166,31 +235,69 @@ def tile_bidirectionalattention_pa_kernel(tc, Q, K, V, cos_t, sin_t, out):
                 start=True,
                 stop=True,
             )
+            state[("o", u)] = o_ps
+
+        def store(u):
+            which, tau, h = units[u]
+            o_ps = state[("o", u)]
             o_sb = spool.tile([P, D], F32, name="o_sb")
             nc.scalar.copy(out=o_sb[:], in_=o_ps[:])
             r0 = h * T + tau * P
             nc.sync.dma_start(out=outf[r0 : r0 + P, :], in_=o_sb[:])
 
-        load_tables(0)
-        load(0)
-        load(1)
-        nc.scalar.dma_start(out=v_raw[:], in_=Vf.rearrange("(j p) d -> p j d", p=P))
-        nc.scalar.copy(out=v_grp[:], in_=v_raw[:].rearrange("p j d -> p d j"))
-        nc.vector.quantize_mx(
-            out=vcodes[:].bitcast(FP8X4), scales=vscales[:], in_=v_grp[:].rearrange("p d j -> p (d j)")
-        )
+        def is_q(u):
+            return 0 <= u < NU and units[u][0] == 1
 
-        for s in range(NU + 2):
-            if s + 2 < NU:
-                which, tau, h = units[s + 2]
-                if which == 0 and h == 0 and tau > 0:
-                    load_tables(tau)
-                load(s + 2)
-            if s < NU:
-                products(s)
-                rotate_sum(s)
-            if 0 <= s - 1 < NU:
-                quantise(s - 1)
-                scores(s - 1)
+        nc.sync.dma_start(out=cos_sb[0][:], in_=cos_t[0:P, :])
+        load(0)
+        nc.sync.dma_start(out=sin_sb[0][:], in_=sin_t[0:P, :])
+        for u in range(1, AHEAD):
+            load(u)
+        nc.scalar.dma_start(out=v_raw[:], in_=Vf.rearrange("(j p) d -> p j d", p=P))
+        negate_sin(0)
+        tables_flip(0)
+        for part in range(3):
+            tables_back(0, part)
+
+        for s in range(NU + 4):
+            if s < NU and units[s][0] == 0 and units[s][2] == 0 and units[s][1] + 1 < TT:
+                load_tables(units[s][1] + 1)
+            if s + AHEAD < NU:
+                load(s + AHEAD)
+            last_of_phase = s < NU - 1 and units[s][2] == H - 1
+            next_tau = units[s + 1][1] if s < NU - 1 else 0
             if 0 <= s - 2 < NU:
-                output(s - 2)
+                quantise(s - 2)
+            if s < NU:
+                products_begin(s)
+                product_sin_gpsimd(s)
+                product_cos(s, 0)
+            if is_q(s - 3):
+                scores_quantise(s - 3)
+            if s < NU:
+                product_cos(s, 1)
+                product_sin_vector(s)
+            if s == 2:
+                nc.scalar.copy(out=v_grp[:], in_=v_raw[:].rearrange("p j d -> p d j"))
+            if s == 4:
+                nc.vector.quantize_mx(
+                    out=vcodes[:].bitcast(FP8X4), scales=vscales[:], in_=v_grp[:].rearrange("p d j -> p (d j)")
+                )
+            if s < NU and units[s][0] == 0 and units[s][2] == 2 and units[s][1] + 1 < TT:
+                negate_sin(units[s][1] + 1)
+                tables_flip(units[s][1] + 1)
+            if 0 <= s - 1 < NU:
+                rotate_sum(s - 1)
+            if last_of_phase:
+                tables_back(next_tau, 0)
+                tables_back(next_tau, 1)
+            if is_q(s - 2):
+                scores(s - 2)
+            if is_q(s - 3):
+                values(s - 3)
+            if last_of_phase:
+                tables_back(next_tau, 2)
+            if is_q(s - 2):
+                scores_out(s - 2)
+            if is_q(s - 3):
+                store(s - 3)

@@ -157,24 +157,30 @@ def tile_bidirectionalattention_pa_kernel(tc, Q, K, V, cos_t, sin_t, out):
             nc.gpsimd.tensor_tensor(out=b[:, 0, NB:NI], in0=xv[:, 1, NB:NI], in1=sneg[tau][:], op=MULT)
             nc.gpsimd.tensor_tensor(out=b[:, 1, NB:NI], in0=xv[:, 0, NB:NI], in1=sv[:, 1, NB:NI], op=MULT)
 
-        def rotate_sum(u):
+        def rotate_sum(u, banks, plain):
             a, b = state[("ab", u)]
-            grp = gpool.tile([P, NG, P, 4], BF16, name="grp", align_bytes=64)
-            for g in range(NG):
+            if banks[0] == 0:
+                state[("grp", u)] = gpool.tile([P, NG, P, 4], BF16, name="grp", align_bytes=64)
+            grp = state[("grp", u)]
+            for g in banks:
                 ps = accp.tile([P, 4, P], F32, name="ps")
-                for half in range(2):
-                    for e in range(2):
-                        c = 2 * g + half
-                        cols = slice(c * P, (c + 1) * P)
-                        dst = ps[:, 2 * half + e, :]
-                        nc.tensor.matmul(
-                            out=dst, lhsT=a[:, e, cols], rhs=ident[:], start=True, stop=False, is_transpose=True
-                        )
+                n_plain = 4 if (plain > 0 and g == 0 and units[u][2] == 0) else plain
+                for j in range(4):
+                    half = j // 2
+                    e = j % 2
+                    c = 2 * g + half
+                    cols = slice(c * P, (c + 1) * P)
+                    dst = ps[:, j, :]
+                    nc.tensor.matmul(
+                        out=dst, lhsT=a[:, e, cols], rhs=ident[:], start=True, stop=False, is_transpose=True
+                    )
+                    if j >= 4 - n_plain:
+                        nc.tensor.matmul(out=dst, lhsT=b[:, e, cols], rhs=ident[:], start=False, stop=True)
+                    else:
                         nc.tensor.matmul(
                             out=dst, lhsT=b[:, e, cols], rhs=ident[:], start=False, stop=True, is_transpose=True
                         )
                 nc.scalar.copy(out=grp[:, g, :, :], in_=ps[:].rearrange("p j t -> p t j"))
-            state[("grp", u)] = grp
 
         def quantise(u):
             which, tau, h = units[u]
@@ -192,11 +198,13 @@ def tile_bidirectionalattention_pa_kernel(tc, Q, K, V, cos_t, sin_t, out):
                 out=codes.bitcast(FP8X4), scales=scales, in_=grp[:].rearrange("p g t j -> p (g t j)")
             )
 
-        def scores(u):
+        def scores(u, key_tiles):
             which, tau, h = units[u]
             qc, qs = state[("q", u)]
-            sc = scp.tile([P, TT, P], F32, name="sc")
-            for tk in range(TT):
+            if key_tiles[0] == 0:
+                state[("sc", u)] = scp.tile([P, TT, P], F32, name="sc")
+            sc = state[("sc", u)]
+            for tk in key_tiles:
                 for g in range(NG):
                     cols = slice(g * P, (g + 1) * P)
                     nc.tensor.matmul_mx(
@@ -208,7 +216,6 @@ def tile_bidirectionalattention_pa_kernel(tc, Q, K, V, cos_t, sin_t, out):
                         start=(g == 0),
                         stop=(g == NG - 1),
                     )
-            state[("sc", u)] = sc
 
         def scores_out(u):
             sc = state[("sc", u)]
@@ -286,13 +293,18 @@ def tile_bidirectionalattention_pa_kernel(tc, Q, K, V, cos_t, sin_t, out):
             if s < NU and units[s][0] == 0 and units[s][2] == 2 and units[s][1] + 1 < TT:
                 negate_sin(units[s][1] + 1)
                 tables_flip(units[s][1] + 1)
+            plain = 0 if is_q(s - 2) else 1
             if 0 <= s - 1 < NU:
-                rotate_sum(s - 1)
+                rotate_sum(s - 1, (0, 1), plain)
+            if is_q(s - 2):
+                scores(s - 2, (0, 1))
+            if 0 <= s - 1 < NU:
+                rotate_sum(s - 1, (2, 3), plain)
             if last_of_phase:
                 tables_back(next_tau, 0)
                 tables_back(next_tau, 1)
             if is_q(s - 2):
-                scores(s - 2)
+                scores(s - 2, (2, 3))
             if is_q(s - 3):
                 values(s - 3)
             if last_of_phase:

@@ -42,9 +42,8 @@ def tile_bidirectionalattention_pa_kernel(tc, Q, K, V, cos_t, sin_t, out):
         qpool = ctx.enter_context(tc.tile_pool(name="qpool", bufs=2))
         spool = ctx.enter_context(tc.tile_pool(name="spool", bufs=2))
         tabp = ctx.enter_context(tc.psum_pool(name="tabp", bufs=1))
-        accp = ctx.enter_context(tc.psum_pool(name="accp", bufs=3))
+        accp = ctx.enter_context(tc.psum_pool(name="accp", bufs=4))
         scp = ctx.enter_context(tc.psum_pool(name="scp", bufs=1))
-        op = ctx.enter_context(tc.psum_pool(name="op", bufs=1))
         ctx.enter_context(tc.manual_schedule())
 
         ident = const.tile([P, P], F32, name="ident")
@@ -157,30 +156,30 @@ def tile_bidirectionalattention_pa_kernel(tc, Q, K, V, cos_t, sin_t, out):
             nc.gpsimd.tensor_tensor(out=b[:, 0, NB:NI], in0=xv[:, 1, NB:NI], in1=sneg[tau][:], op=MULT)
             nc.gpsimd.tensor_tensor(out=b[:, 1, NB:NI], in0=xv[:, 0, NB:NI], in1=sv[:, 1, NB:NI], op=MULT)
 
-        def rotate_sum(u, banks, plain):
+        def rotate_sum(u):
             a, b = state[("ab", u)]
-            if banks[0] == 0:
-                state[("grp", u)] = gpool.tile([P, NG, P, 4], BF16, name="grp", align_bytes=64)
-            grp = state[("grp", u)]
-            for g in banks:
-                ps = accp.tile([P, 4, P], F32, name="ps")
-                n_plain = 4 if (plain > 0 and g == 0 and units[u][2] == 0) else plain
+            grp = gpool.tile([P, NG, P, 4], BF16, name="grp", align_bytes=64)
+            for g0 in range(0, NG, 2):
+                pair = []
+                for g in (g0, g0 + 1):
+                    ps = accp.tile([P, 4, P], F32, name="ps")
+                    pair.append((g, ps))
                 for j in range(4):
-                    half = j // 2
                     e = j % 2
-                    c = 2 * g + half
-                    cols = slice(c * P, (c + 1) * P)
-                    dst = ps[:, j, :]
-                    nc.tensor.matmul(
-                        out=dst, lhsT=a[:, e, cols], rhs=ident[:], start=True, stop=False, is_transpose=True
-                    )
-                    if j >= 4 - n_plain:
-                        nc.tensor.matmul(out=dst, lhsT=b[:, e, cols], rhs=ident[:], start=False, stop=True)
-                    else:
-                        nc.tensor.matmul(
-                            out=dst, lhsT=b[:, e, cols], rhs=ident[:], start=False, stop=True, is_transpose=True
-                        )
-                nc.scalar.copy(out=grp[:, g, :, :], in_=ps[:].rearrange("p j t -> p t j"))
+                    for src, first in ((a, True), (b, False)):
+                        for g, ps in pair:
+                            c = 2 * g + j // 2
+                            nc.tensor.matmul(
+                                out=ps[:, j, :],
+                                lhsT=src[:, e, c * P : (c + 1) * P],
+                                rhs=ident[:],
+                                start=first,
+                                stop=not first,
+                                is_transpose=True,
+                            )
+                for g, ps in pair:
+                    nc.scalar.copy(out=grp[:, g, :, :], in_=ps[:].rearrange("p j t -> p t j"))
+            state[("grp", u)] = grp
 
         def quantise(u):
             which, tau, h = units[u]
@@ -198,13 +197,11 @@ def tile_bidirectionalattention_pa_kernel(tc, Q, K, V, cos_t, sin_t, out):
                 out=codes.bitcast(FP8X4), scales=scales, in_=grp[:].rearrange("p g t j -> p (g t j)")
             )
 
-        def scores(u, key_tiles):
+        def scores(u):
             which, tau, h = units[u]
             qc, qs = state[("q", u)]
-            if key_tiles[0] == 0:
-                state[("sc", u)] = scp.tile([P, TT, P], F32, name="sc")
-            sc = state[("sc", u)]
-            for tk in key_tiles:
+            sc = scp.tile([P, TT, P], F32, name="sc")
+            for tk in range(TT):
                 for g in range(NG):
                     cols = slice(g * P, (g + 1) * P)
                     nc.tensor.matmul_mx(
@@ -216,6 +213,7 @@ def tile_bidirectionalattention_pa_kernel(tc, Q, K, V, cos_t, sin_t, out):
                         start=(g == 0),
                         stop=(g == NG - 1),
                     )
+            state[("sc", u)] = sc
 
         def scores_out(u):
             sc = state[("sc", u)]
@@ -232,9 +230,10 @@ def tile_bidirectionalattention_pa_kernel(tc, Q, K, V, cos_t, sin_t, out):
 
         def values(u):
             scd, ssc = state[("scd", u)]
-            o_ps = op.tile([P, D], F32, name="o_ps")
+            ps = accp.tile([P, 4, P], F32, name="ps")
+            o_ps = ps[:].rearrange("p j t -> p (j t)")[:, 0:D]
             nc.tensor.matmul_mx(
-                out=o_ps[:],
+                out=o_ps,
                 lhsT=scd[:].bitcast(FP8X4),
                 lhsT_scale=ssc[:],
                 rhs=vcodes[:].bitcast(FP8X4),
@@ -248,7 +247,7 @@ def tile_bidirectionalattention_pa_kernel(tc, Q, K, V, cos_t, sin_t, out):
             which, tau, h = units[u]
             o_ps = state[("o", u)]
             o_sb = spool.tile([P, D], F32, name="o_sb")
-            nc.scalar.copy(out=o_sb[:], in_=o_ps[:])
+            nc.scalar.copy(out=o_sb[:], in_=o_ps)
             r0 = h * T + tau * P
             nc.sync.dma_start(out=outf[r0 : r0 + P, :], in_=o_sb[:])
 
@@ -293,18 +292,13 @@ def tile_bidirectionalattention_pa_kernel(tc, Q, K, V, cos_t, sin_t, out):
             if s < NU and units[s][0] == 0 and units[s][2] == 2 and units[s][1] + 1 < TT:
                 negate_sin(units[s][1] + 1)
                 tables_flip(units[s][1] + 1)
-            plain = 0 if is_q(s - 2) else 1
             if 0 <= s - 1 < NU:
-                rotate_sum(s - 1, (0, 1), plain)
-            if is_q(s - 2):
-                scores(s - 2, (0, 1))
-            if 0 <= s - 1 < NU:
-                rotate_sum(s - 1, (2, 3), plain)
+                rotate_sum(s - 1)
             if last_of_phase:
                 tables_back(next_tau, 0)
                 tables_back(next_tau, 1)
             if is_q(s - 2):
-                scores(s - 2, (2, 3))
+                scores(s - 2)
             if is_q(s - 3):
                 values(s - 3)
             if last_of_phase:

@@ -19,10 +19,12 @@ D = 256
 TT = T // P
 NG = N // 512
 NI = N // 2
-NB = 384
+NB = 640
 NBB = NB // P
 NTB = 8 + NBB
 AHEAD = 3
+NA = (1, 2)
+ADD = mybir.AluOpType.add
 FLOPS = 2 * H * T * T * N + 2 * H * T * T * D
 
 
@@ -42,12 +44,15 @@ def tile_bidirectionalattention_pa_kernel(tc, Q, K, V, cos_t, sin_t, out):
         qpool = ctx.enter_context(tc.tile_pool(name="qpool", bufs=2))
         spool = ctx.enter_context(tc.tile_pool(name="spool", bufs=2))
         tabp = ctx.enter_context(tc.psum_pool(name="tabp", bufs=1))
-        accp = ctx.enter_context(tc.psum_pool(name="accp", bufs=4))
+        accp = ctx.enter_context(tc.psum_pool(name="accp", bufs=3))
         scp = ctx.enter_context(tc.psum_pool(name="scp", bufs=1))
+        rpool = ctx.enter_context(tc.tile_pool(name="rpool", bufs=2))
         ctx.enter_context(tc.manual_schedule())
 
         ident = const.tile([P, P], F32, name="ident")
         make_identity(nc, ident[:])
+        ident_bf = const.tile([P, P], BF16, name="ident_bf")
+        make_identity(nc, ident_bf[:])
 
         cos_sb = []
         sin_sb = []
@@ -103,15 +108,10 @@ def tile_bidirectionalattention_pa_kernel(tc, Q, K, V, cos_t, sin_t, out):
                 nc.scalar.copy(out=tab_t[tau][:, b0 : b0 + n, :], in_=ps[:, 0:n, :])
 
         def tables_back(tau, part):
-            if part == 0:
-                t = tabp.tile([P, 512], F32, name="tabc0")
-                blocks = range(0, 4)
-            elif part == 1:
-                t = tabp.tile([P, 512], F32, name="tabc1")
-                blocks = range(4, 8)
-            else:
-                t = tabp.tile([P, 512], F32, name="tabs")
-                blocks = range(8, NTB)
+            blocks = range(4 * part, min(4 * part + 4, NTB))
+            if len(blocks) == 0:
+                return
+            t = tabp.tile([P, 512], F32, name="tab%d" % part)
             for k, b in enumerate(blocks):
                 nc.tensor.transpose(t[:, k * P : (k + 1) * P], tab_t[tau][:, b, :], ident[:])
             state[("tab", part)] = t
@@ -139,14 +139,18 @@ def tile_bidirectionalattention_pa_kernel(tc, Q, K, V, cos_t, sin_t, out):
             which, tau, h = units[u]
             xv = pair_view(state[("x", u)][:])
             a, b = state[("ab", u)]
-            if u == 0:
-                sv = pair_view(sin_sb[tau][:])[:, :, 0:NB]
-            else:
-                sv = pair_view(state[("tab", 2)][:].bitcast(BF16)[:, 0 : 2 * NB])
-            nc.vector.scalar_tensor_tensor(
-                out=b[:, 0, 0:NB], in0=xv[:, 1, 0:NB], scalar=-1.0, in1=sv[:, 0, :], op0=MULT, op1=MULT
-            )
-            nc.vector.tensor_tensor(out=b[:, 1, 0:NB], in0=xv[:, 0, 0:NB], in1=sv[:, 1, :], op=MULT)
+            for part, lo in ((2, 0), (3, 512)):
+                hi = min(NB, lo + 512)
+                if hi <= lo:
+                    continue
+                if u == 0:
+                    sv = pair_view(sin_sb[tau][:])[:, :, lo:hi]
+                else:
+                    sv = pair_view(state[("tab", part)][:].bitcast(BF16)[:, 0 : 2 * (hi - lo)])
+                nc.vector.scalar_tensor_tensor(
+                    out=b[:, 0, lo:hi], in0=xv[:, 1, lo:hi], scalar=-1.0, in1=sv[:, 0, :], op0=MULT, op1=MULT
+                )
+                nc.vector.tensor_tensor(out=b[:, 1, lo:hi], in0=xv[:, 0, lo:hi], in1=sv[:, 1, :], op=MULT)
 
         def product_sin_gpsimd(u):
             which, tau, h = units[u]
@@ -156,29 +160,39 @@ def tile_bidirectionalattention_pa_kernel(tc, Q, K, V, cos_t, sin_t, out):
             nc.gpsimd.tensor_tensor(out=b[:, 0, NB:NI], in0=xv[:, 1, NB:NI], in1=sneg[tau][:], op=MULT)
             nc.gpsimd.tensor_tensor(out=b[:, 1, NB:NI], in0=xv[:, 0, NB:NI], in1=sv[:, 1, NB:NI], op=MULT)
 
+        def add_gpsimd(u):
+            n_add = NA[units[u][0]]
+            if n_add == 0:
+                return
+            a, b = state[("ab", u)]
+            lo = NI - 256 * n_add
+            r = rpool.tile([P, 2, 256 * n_add], BF16, name="r")
+            nc.gpsimd.tensor_tensor(out=r[:], in0=a[:, :, lo:NI], in1=b[:, :, lo:NI], op=ADD)
+            state[("r", u)] = r
+
         def rotate_sum(u):
             a, b = state[("ab", u)]
+            n_add = NA[units[u][0]]
             grp = gpool.tile([P, NG, P, 4], BF16, name="grp", align_bytes=64)
-            for g0 in range(0, NG, 2):
-                pair = []
-                for g in (g0, g0 + 1):
+            for g in range(NG):
+                if g < NG - n_add:
                     ps = accp.tile([P, 4, P], F32, name="ps")
-                    pair.append((g, ps))
-                for j in range(4):
-                    e = j % 2
-                    for src, first in ((a, True), (b, False)):
-                        for g, ps in pair:
-                            c = 2 * g + j // 2
-                            nc.tensor.matmul(
-                                out=ps[:, j, :],
-                                lhsT=src[:, e, c * P : (c + 1) * P],
-                                rhs=ident[:],
-                                start=first,
-                                stop=not first,
-                                is_transpose=True,
-                            )
-                for g, ps in pair:
-                    nc.scalar.copy(out=grp[:, g, :, :], in_=ps[:].rearrange("p j t -> p t j"))
+                    for j in range(4):
+                        c = 2 * g + j // 2
+                        cols = slice(c * P, (c + 1) * P)
+                        nc.tensor.matmul(
+                            out=ps[:, j, :], lhsT=a[:, j % 2, cols], rhs=ident[:], start=True, stop=False, is_transpose=True
+                        )
+                        nc.tensor.matmul(
+                            out=ps[:, j, :], lhsT=b[:, j % 2, cols], rhs=ident[:], start=False, stop=True, is_transpose=True
+                        )
+                else:
+                    r = state[("r", u)]
+                    ps = accp.tile([P, 4, P], BF16, name="ps")
+                    for j in range(4):
+                        c = 2 * (g - (NG - n_add)) + j // 2
+                        nc.tensor.transpose(ps[:, j, :], r[:, j % 2, c * P : (c + 1) * P], ident_bf[:])
+                nc.scalar.copy(out=grp[:, g, :, :], in_=ps[:].rearrange("p j t -> p t j"))
             state[("grp", u)] = grp
 
         def quantise(u):
@@ -262,7 +276,7 @@ def tile_bidirectionalattention_pa_kernel(tc, Q, K, V, cos_t, sin_t, out):
         nc.scalar.dma_start(out=v_raw[:], in_=Vf.rearrange("(j p) d -> p j d", p=P))
         negate_sin(0)
         tables_flip(0)
-        for part in range(3):
+        for part in range(4):
             tables_back(0, part)
 
         for s in range(NU + 4):
@@ -274,6 +288,8 @@ def tile_bidirectionalattention_pa_kernel(tc, Q, K, V, cos_t, sin_t, out):
             next_tau = units[s + 1][1] if s < NU - 1 else 0
             if 0 <= s - 2 < NU:
                 quantise(s - 2)
+            if 0 <= s - 1 < NU:
+                add_gpsimd(s - 1)
             if s < NU:
                 products_begin(s)
                 product_sin_gpsimd(s)
@@ -303,6 +319,7 @@ def tile_bidirectionalattention_pa_kernel(tc, Q, K, V, cos_t, sin_t, out):
                 values(s - 3)
             if last_of_phase:
                 tables_back(next_tau, 2)
+                tables_back(next_tau, 3)
             if is_q(s - 2):
                 scores_out(s - 2)
             if is_q(s - 3):

@@ -19,12 +19,10 @@ D = 256
 TT = T // P
 NG = N // 512
 NI = N // 2
-NB = 640
+NB = 384
 NBB = NB // P
 NTB = 8 + NBB
 AHEAD = 3
-NA = (1, 2)
-ADD = mybir.AluOpType.add
 FLOPS = 2 * H * T * T * N + 2 * H * T * T * D
 
 
@@ -46,13 +44,11 @@ def tile_bidirectionalattention_pa_kernel(tc, Q, K, V, cos_t, sin_t, out):
         tabp = ctx.enter_context(tc.psum_pool(name="tabp", bufs=1))
         accp = ctx.enter_context(tc.psum_pool(name="accp", bufs=3))
         scp = ctx.enter_context(tc.psum_pool(name="scp", bufs=1))
-        rpool = ctx.enter_context(tc.tile_pool(name="rpool", bufs=2))
+        op = ctx.enter_context(tc.psum_pool(name="op", bufs=1))
         ctx.enter_context(tc.manual_schedule())
 
         ident = const.tile([P, P], F32, name="ident")
         make_identity(nc, ident[:])
-        ident_bf = const.tile([P, P], BF16, name="ident_bf")
-        make_identity(nc, ident_bf[:])
 
         cos_sb = []
         sin_sb = []
@@ -108,10 +104,15 @@ def tile_bidirectionalattention_pa_kernel(tc, Q, K, V, cos_t, sin_t, out):
                 nc.scalar.copy(out=tab_t[tau][:, b0 : b0 + n, :], in_=ps[:, 0:n, :])
 
         def tables_back(tau, part):
-            blocks = range(4 * part, min(4 * part + 4, NTB))
-            if len(blocks) == 0:
-                return
-            t = tabp.tile([P, 512], F32, name="tab%d" % part)
+            if part == 0:
+                t = tabp.tile([P, 512], F32, name="tabc0")
+                blocks = range(0, 4)
+            elif part == 1:
+                t = tabp.tile([P, 512], F32, name="tabc1")
+                blocks = range(4, 8)
+            else:
+                t = tabp.tile([P, 512], F32, name="tabs")
+                blocks = range(8, NTB)
             for k, b in enumerate(blocks):
                 nc.tensor.transpose(t[:, k * P : (k + 1) * P], tab_t[tau][:, b, :], ident[:])
             state[("tab", part)] = t
@@ -139,18 +140,14 @@ def tile_bidirectionalattention_pa_kernel(tc, Q, K, V, cos_t, sin_t, out):
             which, tau, h = units[u]
             xv = pair_view(state[("x", u)][:])
             a, b = state[("ab", u)]
-            for part, lo in ((2, 0), (3, 512)):
-                hi = min(NB, lo + 512)
-                if hi <= lo:
-                    continue
-                if u == 0:
-                    sv = pair_view(sin_sb[tau][:])[:, :, lo:hi]
-                else:
-                    sv = pair_view(state[("tab", part)][:].bitcast(BF16)[:, 0 : 2 * (hi - lo)])
-                nc.vector.scalar_tensor_tensor(
-                    out=b[:, 0, lo:hi], in0=xv[:, 1, lo:hi], scalar=-1.0, in1=sv[:, 0, :], op0=MULT, op1=MULT
-                )
-                nc.vector.tensor_tensor(out=b[:, 1, lo:hi], in0=xv[:, 0, lo:hi], in1=sv[:, 1, :], op=MULT)
+            if u == 0:
+                sv = pair_view(sin_sb[tau][:])[:, :, 0:NB]
+            else:
+                sv = pair_view(state[("tab", 2)][:].bitcast(BF16)[:, 0 : 2 * NB])
+            nc.vector.scalar_tensor_tensor(
+                out=b[:, 0, 0:NB], in0=xv[:, 1, 0:NB], scalar=-1.0, in1=sv[:, 0, :], op0=MULT, op1=MULT
+            )
+            nc.vector.tensor_tensor(out=b[:, 1, 0:NB], in0=xv[:, 0, 0:NB], in1=sv[:, 1, :], op=MULT)
 
         def product_sin_gpsimd(u):
             which, tau, h = units[u]
@@ -160,38 +157,22 @@ def tile_bidirectionalattention_pa_kernel(tc, Q, K, V, cos_t, sin_t, out):
             nc.gpsimd.tensor_tensor(out=b[:, 0, NB:NI], in0=xv[:, 1, NB:NI], in1=sneg[tau][:], op=MULT)
             nc.gpsimd.tensor_tensor(out=b[:, 1, NB:NI], in0=xv[:, 0, NB:NI], in1=sv[:, 1, NB:NI], op=MULT)
 
-        def add_gpsimd(u):
-            n_add = NA[units[u][0]]
-            if n_add == 0:
-                return
-            a, b = state[("ab", u)]
-            lo = NI - 256 * n_add
-            r = rpool.tile([P, 2, 256 * n_add], BF16, name="r")
-            nc.gpsimd.tensor_tensor(out=r[:], in0=a[:, :, lo:NI], in1=b[:, :, lo:NI], op=ADD)
-            state[("r", u)] = r
-
         def rotate_sum(u):
             a, b = state[("ab", u)]
-            n_add = NA[units[u][0]]
             grp = gpool.tile([P, NG, P, 4], BF16, name="grp", align_bytes=64)
             for g in range(NG):
-                if g < NG - n_add:
-                    ps = accp.tile([P, 4, P], F32, name="ps")
-                    for j in range(4):
-                        c = 2 * g + j // 2
+                ps = accp.tile([P, 4, P], F32, name="ps")
+                for half in range(2):
+                    for e in range(2):
+                        c = 2 * g + half
                         cols = slice(c * P, (c + 1) * P)
+                        dst = ps[:, 2 * half + e, :]
                         nc.tensor.matmul(
-                            out=ps[:, j, :], lhsT=a[:, j % 2, cols], rhs=ident[:], start=True, stop=False, is_transpose=True
+                            out=dst, lhsT=a[:, e, cols], rhs=ident[:], start=True, stop=False, is_transpose=True
                         )
                         nc.tensor.matmul(
-                            out=ps[:, j, :], lhsT=b[:, j % 2, cols], rhs=ident[:], start=False, stop=True, is_transpose=True
+                            out=dst, lhsT=b[:, e, cols], rhs=ident[:], start=False, stop=True, is_transpose=True
                         )
-                else:
-                    r = state[("r", u)]
-                    ps = accp.tile([P, 4, P], BF16, name="ps")
-                    for j in range(4):
-                        c = 2 * (g - (NG - n_add)) + j // 2
-                        nc.tensor.transpose(ps[:, j, :], r[:, j % 2, c * P : (c + 1) * P], ident_bf[:])
                 nc.scalar.copy(out=grp[:, g, :, :], in_=ps[:].rearrange("p j t -> p t j"))
             state[("grp", u)] = grp
 
@@ -244,10 +225,9 @@ def tile_bidirectionalattention_pa_kernel(tc, Q, K, V, cos_t, sin_t, out):
 
         def values(u):
             scd, ssc = state[("scd", u)]
-            ps = accp.tile([P, 4, P], F32, name="ps")
-            o_ps = ps[:].rearrange("p j t -> p (j t)")[:, 0:D]
+            o_ps = op.tile([P, D], F32, name="o_ps")
             nc.tensor.matmul_mx(
-                out=o_ps,
+                out=o_ps[:],
                 lhsT=scd[:].bitcast(FP8X4),
                 lhsT_scale=ssc[:],
                 rhs=vcodes[:].bitcast(FP8X4),
@@ -261,7 +241,7 @@ def tile_bidirectionalattention_pa_kernel(tc, Q, K, V, cos_t, sin_t, out):
             which, tau, h = units[u]
             o_ps = state[("o", u)]
             o_sb = spool.tile([P, D], F32, name="o_sb")
-            nc.scalar.copy(out=o_sb[:], in_=o_ps)
+            nc.scalar.copy(out=o_sb[:], in_=o_ps[:])
             r0 = h * T + tau * P
             nc.sync.dma_start(out=outf[r0 : r0 + P, :], in_=o_sb[:])
 
@@ -274,9 +254,14 @@ def tile_bidirectionalattention_pa_kernel(tc, Q, K, V, cos_t, sin_t, out):
         for u in range(1, AHEAD):
             load(u)
         nc.scalar.dma_start(out=v_raw[:], in_=Vf.rearrange("(j p) d -> p j d", p=P))
+        nc.scalar.copy(out=v_grp[:], in_=v_raw[:].rearrange("p j d -> p d j"))
+        nc.vector.quantize_mx(
+            out=vcodes[:].bitcast(FP8X4), scales=vscales[:], in_=v_grp[:].rearrange("p d j -> p (d j)")
+        )
+        idle = scp.tile([P, TT, P], F32, name="sc")
         negate_sin(0)
         tables_flip(0)
-        for part in range(4):
+        for part in range(3):
             tables_back(0, part)
 
         for s in range(NU + 4):
@@ -288,8 +273,6 @@ def tile_bidirectionalattention_pa_kernel(tc, Q, K, V, cos_t, sin_t, out):
             next_tau = units[s + 1][1] if s < NU - 1 else 0
             if 0 <= s - 2 < NU:
                 quantise(s - 2)
-            if 0 <= s - 1 < NU:
-                add_gpsimd(s - 1)
             if s < NU:
                 products_begin(s)
                 product_sin_gpsimd(s)
@@ -299,12 +282,6 @@ def tile_bidirectionalattention_pa_kernel(tc, Q, K, V, cos_t, sin_t, out):
             if s < NU:
                 product_cos(s, 1)
                 product_sin_vector(s)
-            if s == 2:
-                nc.scalar.copy(out=v_grp[:], in_=v_raw[:].rearrange("p j d -> p d j"))
-            if s == 4:
-                nc.vector.quantize_mx(
-                    out=vcodes[:].bitcast(FP8X4), scales=vscales[:], in_=v_grp[:].rearrange("p d j -> p (d j)")
-                )
             if s < NU and units[s][0] == 0 and units[s][2] == 2 and units[s][1] + 1 < TT:
                 negate_sin(units[s][1] + 1)
                 tables_flip(units[s][1] + 1)
@@ -315,11 +292,21 @@ def tile_bidirectionalattention_pa_kernel(tc, Q, K, V, cos_t, sin_t, out):
                 tables_back(next_tau, 1)
             if is_q(s - 2):
                 scores(s - 2)
+            elif 0 <= s - 1 < NU:
+                for k in range(16):
+                    nc.tensor.matmul_mx(
+                        out=idle[:, k % 4, :],
+                        lhsT=vcodes[:, 0:P].bitcast(FP8X4),
+                        lhsT_scale=vscales[:, 0:P],
+                        rhs=vcodes[:, P : 2 * P].bitcast(FP8X4),
+                        rhs_scale=vscales[:, P : 2 * P],
+                        start=True,
+                        stop=True,
+                    )
             if is_q(s - 3):
                 values(s - 3)
             if last_of_phase:
                 tables_back(next_tau, 2)
-                tables_back(next_tau, 3)
             if is_q(s - 2):
                 scores_out(s - 2)
             if is_q(s - 3):

@@ -19,11 +19,14 @@ D = 256
 TT = T // P
 NG = N // 512
 NI = N // 2
-NB = 384
-NBB = NB // P
-NTB = 8 + NBB
+NB = 512
+NTB = 8 + NB // P
 AHEAD = 3
 FLOPS = 2 * H * T * T * N + 2 * H * T * T * D
+
+
+def pair_view(ap):
+    return ap.rearrange("p (i e) -> p e i", e=2)
 
 
 def tile_bidirectionalattention_pa_kernel(tc, Q, K, V, cos_t, sin_t, out):
@@ -34,30 +37,46 @@ def tile_bidirectionalattention_pa_kernel(tc, Q, K, V, cos_t, sin_t, out):
     outf = out.flatten_outer_dims()
     inv_sqrt_n = 1.0 / (float(N) ** 0.5)
 
+    units = []
+    for tau in range(TT):
+        units.append((0, tau, 0, True))
+    for h in range(H - 1):
+        for tau in range(TT):
+            units.append((1, tau, h, False))
+            units.append((0, tau, h + 1, False))
+    for tau in range(TT):
+        units.append((1, tau, H - 1, True))
+    NU = len(units)
+
+    def is_q(u):
+        return 0 <= u < NU and units[u][0] == 1
+
+    def spread(u):
+        return is_q(u) and u + 1 < NU and units[u + 1][0] == 0
+
     with ExitStack() as ctx:
         const = ctx.enter_context(tc.tile_pool(name="const", bufs=1))
+        rawp = ctx.enter_context(tc.tile_pool(name="rawp", bufs=2))
         xpool = ctx.enter_context(tc.tile_pool(name="xpool", bufs=AHEAD + 1))
         prod = ctx.enter_context(tc.tile_pool(name="prod", bufs=3))
         gpool = ctx.enter_context(tc.tile_pool(name="gpool", bufs=3))
         qpool = ctx.enter_context(tc.tile_pool(name="qpool", bufs=2))
         spool = ctx.enter_context(tc.tile_pool(name="spool", bufs=2))
         tabp = ctx.enter_context(tc.psum_pool(name="tabp", bufs=1))
-        accp = ctx.enter_context(tc.psum_pool(name="accp", bufs=3))
+        accp = ctx.enter_context(tc.psum_pool(name="accp", bufs=4))
         scp = ctx.enter_context(tc.psum_pool(name="scp", bufs=1))
-        op = ctx.enter_context(tc.psum_pool(name="op", bufs=1))
         ctx.enter_context(tc.manual_schedule())
 
         ident = const.tile([P, P], F32, name="ident")
         make_identity(nc, ident[:])
-
         cos_sb = []
-        sin_sb = []
-        sneg = []
+        sin_lo = []
+        sin_hi = []
         tab_t = []
         for tau in range(TT):
             cos_sb.append(const.tile([P, N], BF16, name="cos%d" % tau))
-            sin_sb.append(const.tile([P, N], BF16, name="sin%d" % tau))
-            sneg.append(const.tile([P, NI - NB], BF16, name="sneg%d" % tau))
+            sin_lo.append(const.tile([P, 2 * NB], BF16, name="sinlo%d" % tau))
+            sin_hi.append(const.tile([P, 2, NI - NB], BF16, name="sinhi%d" % tau))
             tab_t.append(const.tile([P, NTB, P], F32, name="tabt%d" % tau))
         kcodes = const.tile([P, H * TT, 512], U32, name="kcodes", align_bytes=64)
         kscales = const.tile([P, H * TT, 512], U8, name="kscales", align_bytes=64)
@@ -65,150 +84,123 @@ def tile_bidirectionalattention_pa_kernel(tc, Q, K, V, cos_t, sin_t, out):
         v_grp = const.tile([P, D, 4], BF16, name="v_grp", align_bytes=64)
         vcodes = const.tile([P, D], U32, name="vcodes", align_bytes=64)
         vscales = const.tile([P, D], U8, name="vscales", align_bytes=64)
-
-        units = []
-        for which in range(2):
-            for tau in range(TT):
-                for h in range(H):
-                    units.append((which, tau, h))
-        NU = len(units)
         state = {}
 
         def load_tables(tau):
             rows = slice(tau * P, (tau + 1) * P)
             nc.sync.dma_start(out=cos_sb[tau][:], in_=cos_t[rows, :])
-            nc.sync.dma_start(out=sin_sb[tau][:], in_=sin_t[rows, :])
+            raw = rawp.tile([P, N], BF16, name="sinraw")
+            nc.sync.dma_start(out=raw[:], in_=sin_t[rows, :])
+            state[("sinraw", tau)] = raw
 
         def load(u):
-            which, tau, h = units[u]
-            src = Kf if which == 0 else Qf
+            is_query, tau, h, alone = units[u]
+            src = Qf if is_query else Kf
             x = xpool.tile([P, N], BF16, name="x")
             r0 = h * T + tau * P
             nc.sync.dma_start(out=x[:], in_=src[r0 : r0 + P, :])
             state[("x", u)] = x
 
-        def negate_sin(tau):
-            sv = sin_sb[tau][:].rearrange("p (i e) -> p e i", e=2)
-            nc.scalar.mul(out=sneg[tau][:], in_=sv[:, 0, NB:NI], mul=-1.0)
+        def prepare_sin(tau):
+            sv = pair_view(state[("sinraw", tau)][:])
+            lo = pair_view(sin_lo[tau][:])
+            nc.scalar.copy(out=lo[:, 0, :], in_=sv[:, 1, 0:NB])
+            nc.scalar.mul(out=lo[:, 1, :], in_=sv[:, 0, 0:NB], mul=-1.0)
+            nc.scalar.copy(out=sin_hi[tau][:, 0, :], in_=sv[:, 1, NB:NI])
+            nc.scalar.mul(out=sin_hi[tau][:, 1, :], in_=sv[:, 0, NB:NI], mul=-1.0)
 
         def tables_flip(tau):
             cw = cos_sb[tau][:].bitcast(F32)
-            sw = sin_sb[tau][:].bitcast(F32)
+            sw = sin_lo[tau][:].bitcast(F32)
             for b0 in range(0, NTB, 4):
-                n = min(4, NTB - b0)
                 ps = accp.tile([P, 4, P], F32, name="ps")
-                for k in range(n):
+                for k in range(4):
                     b = b0 + k
                     srcw = cw[:, b * P : (b + 1) * P] if b < 8 else sw[:, (b - 8) * P : (b - 7) * P]
                     nc.tensor.transpose(ps[:, k, :], srcw, ident[:])
-                nc.scalar.copy(out=tab_t[tau][:, b0 : b0 + n, :], in_=ps[:, 0:n, :])
+                nc.scalar.copy(out=tab_t[tau][:, b0 : b0 + 4, :], in_=ps[:])
 
         def tables_back(tau, part):
-            if part == 0:
-                t = tabp.tile([P, 512], F32, name="tabc0")
-                blocks = range(0, 4)
-            elif part == 1:
-                t = tabp.tile([P, 512], F32, name="tabc1")
-                blocks = range(4, 8)
-            else:
-                t = tabp.tile([P, 512], F32, name="tabs")
-                blocks = range(8, NTB)
-            for k, b in enumerate(blocks):
-                nc.tensor.transpose(t[:, k * P : (k + 1) * P], tab_t[tau][:, b, :], ident[:])
+            t = tabp.tile([P, 512], F32, name="tab%d" % part)
+            for k in range(4):
+                nc.tensor.transpose(t[:, k * P : (k + 1) * P], tab_t[tau][:, 4 * part + k, :], ident[:])
             state[("tab", part)] = t
-
-        def pair_view(ap):
-            return ap.rearrange("p (i e) -> p e i", e=2)
 
         def products_begin(u):
             a = prod.tile([P, 2, NI], F32, name="a")
             b = prod.tile([P, 2, NI], F32, name="b")
             state[("ab", u)] = (a, b)
 
-        def product_cos(u, part):
-            which, tau, h = units[u]
+        def product(u, part):
+            is_query, tau, h, alone = units[u]
             xv = pair_view(state[("x", u)][:])
             a, b = state[("ab", u)]
-            rng = slice(part * 512, (part + 1) * 512)
-            if u == 0:
-                cv = pair_view(cos_sb[tau][:])[:, :, rng]
+            rng = slice((part % 2) * 512, (part % 2) * 512 + 512)
+            dst = a if part < 2 else b
+            if part == 3:
+                eng = nc.vector if alone else nc.gpsimd
+                eng.tensor_tensor(out=dst[:, :, rng], in0=xv[:, :, rng], in1=sin_hi[tau][:], op=MULT)
+                return
+            if not alone:
+                tab = pair_view(state[("tab", part)][:].bitcast(BF16))
+            elif part == 2:
+                tab = pair_view(sin_lo[tau][:])
             else:
-                cv = pair_view(state[("tab", part)][:].bitcast(BF16))
-            nc.vector.tensor_tensor(out=a[:, :, rng], in0=xv[:, :, rng], in1=cv, op=MULT)
+                tab = pair_view(cos_sb[tau][:])[:, :, rng]
+            nc.vector.tensor_tensor(out=dst[:, :, rng], in0=xv[:, :, rng], in1=tab, op=MULT)
 
-        def product_sin_vector(u):
-            which, tau, h = units[u]
-            xv = pair_view(state[("x", u)][:])
+        def rotate_sum(u, banks):
             a, b = state[("ab", u)]
-            if u == 0:
-                sv = pair_view(sin_sb[tau][:])[:, :, 0:NB]
-            else:
-                sv = pair_view(state[("tab", 2)][:].bitcast(BF16)[:, 0 : 2 * NB])
-            nc.vector.scalar_tensor_tensor(
-                out=b[:, 0, 0:NB], in0=xv[:, 1, 0:NB], scalar=-1.0, in1=sv[:, 0, :], op0=MULT, op1=MULT
-            )
-            nc.vector.tensor_tensor(out=b[:, 1, 0:NB], in0=xv[:, 0, 0:NB], in1=sv[:, 1, :], op=MULT)
-
-        def product_sin_gpsimd(u):
-            which, tau, h = units[u]
-            xv = pair_view(state[("x", u)][:])
-            sv = pair_view(sin_sb[tau][:])
-            a, b = state[("ab", u)]
-            nc.gpsimd.tensor_tensor(out=b[:, 0, NB:NI], in0=xv[:, 1, NB:NI], in1=sneg[tau][:], op=MULT)
-            nc.gpsimd.tensor_tensor(out=b[:, 1, NB:NI], in0=xv[:, 0, NB:NI], in1=sv[:, 1, NB:NI], op=MULT)
-
-        def rotate_sum(u):
-            a, b = state[("ab", u)]
-            grp = gpool.tile([P, NG, P, 4], BF16, name="grp", align_bytes=64)
-            for g in range(NG):
+            if banks[0] == 0:
+                state[("grp", u)] = gpool.tile([P, NG, P, 4], BF16, name="grp", align_bytes=64)
+            grp = state[("grp", u)]
+            for g in banks:
                 ps = accp.tile([P, 4, P], F32, name="ps")
-                for half in range(2):
-                    for e in range(2):
-                        c = 2 * g + half
-                        cols = slice(c * P, (c + 1) * P)
-                        dst = ps[:, 2 * half + e, :]
-                        nc.tensor.matmul(
-                            out=dst, lhsT=a[:, e, cols], rhs=ident[:], start=True, stop=False, is_transpose=True
-                        )
-                        nc.tensor.matmul(
-                            out=dst, lhsT=b[:, e, cols], rhs=ident[:], start=False, stop=True, is_transpose=True
-                        )
+                for j in range(4):
+                    e = j % 2
+                    c = 2 * g + j // 2
+                    cols = slice(c * P, (c + 1) * P)
+                    nc.tensor.matmul(
+                        out=ps[:, j, :], lhsT=a[:, e, cols], rhs=ident[:], start=True, stop=False, is_transpose=True
+                    )
+                    nc.tensor.matmul(
+                        out=ps[:, j, :], lhsT=b[:, 1 - e, cols], rhs=ident[:], start=False, stop=True, is_transpose=True
+                    )
                 nc.scalar.copy(out=grp[:, g, :, :], in_=ps[:].rearrange("p j t -> p t j"))
-            state[("grp", u)] = grp
 
         def quantise(u):
-            which, tau, h = units[u]
+            is_query, tau, h, alone = units[u]
             grp = state[("grp", u)]
-            if which == 0:
-                codes = kcodes[:, h * TT + tau, :]
-                scales = kscales[:, h * TT + tau, :]
-            else:
+            if is_query:
                 qc = qpool.tile([P, 512], U32, name="qc", align_bytes=64)
                 qs = qpool.tile([P, 512], U8, name="qs", align_bytes=64)
                 codes = qc[:]
                 scales = qs[:]
                 state[("q", u)] = (qc, qs)
+            else:
+                codes = kcodes[:, h * TT + tau, :]
+                scales = kscales[:, h * TT + tau, :]
             nc.vector.quantize_mx(
                 out=codes.bitcast(FP8X4), scales=scales, in_=grp[:].rearrange("p g t j -> p (g t j)")
             )
 
-        def scores(u):
-            which, tau, h = units[u]
+        def scores(u, tk):
+            h = units[u][2]
             qc, qs = state[("q", u)]
-            sc = scp.tile([P, TT, P], F32, name="sc")
-            for tk in range(TT):
-                for g in range(NG):
-                    cols = slice(g * P, (g + 1) * P)
-                    nc.tensor.matmul_mx(
-                        out=sc[:, tk, :],
-                        lhsT=kcodes[:, h * TT + tk, cols].bitcast(FP8X4),
-                        lhsT_scale=kscales[:, h * TT + tk, cols],
-                        rhs=qc[:, cols].bitcast(FP8X4),
-                        rhs_scale=qs[:, cols],
-                        start=(g == 0),
-                        stop=(g == NG - 1),
-                    )
-            state[("sc", u)] = sc
+            if tk == 0:
+                state[("sc", u)] = scp.tile([P, TT, P], F32, name="sc")
+            sc = state[("sc", u)]
+            for g in range(NG):
+                cols = slice(g * P, (g + 1) * P)
+                nc.tensor.matmul_mx(
+                    out=sc[:, tk, :],
+                    lhsT=kcodes[:, h * TT + tk, cols].bitcast(FP8X4),
+                    lhsT_scale=kscales[:, h * TT + tk, cols],
+                    rhs=qc[:, cols].bitcast(FP8X4),
+                    rhs_scale=qs[:, cols],
+                    start=(g == 0),
+                    stop=(g == NG - 1),
+                )
 
         def scores_out(u):
             sc = state[("sc", u)]
@@ -225,9 +217,10 @@ def tile_bidirectionalattention_pa_kernel(tc, Q, K, V, cos_t, sin_t, out):
 
         def values(u):
             scd, ssc = state[("scd", u)]
-            o_ps = op.tile([P, D], F32, name="o_ps")
+            ps = accp.tile([P, 4, P], F32, name="ps")
+            o_ps = ps[:].rearrange("p j t -> p (j t)")[:, 0:D]
             nc.tensor.matmul_mx(
-                out=o_ps[:],
+                out=o_ps,
                 lhsT=scd[:].bitcast(FP8X4),
                 lhsT_scale=ssc[:],
                 rhs=vcodes[:].bitcast(FP8X4),
@@ -238,76 +231,75 @@ def tile_bidirectionalattention_pa_kernel(tc, Q, K, V, cos_t, sin_t, out):
             state[("o", u)] = o_ps
 
         def store(u):
-            which, tau, h = units[u]
-            o_ps = state[("o", u)]
+            is_query, tau, h, alone = units[u]
             o_sb = spool.tile([P, D], F32, name="o_sb")
-            nc.scalar.copy(out=o_sb[:], in_=o_ps[:])
+            nc.scalar.copy(out=o_sb[:], in_=state[("o", u)])
             r0 = h * T + tau * P
             nc.sync.dma_start(out=outf[r0 : r0 + P, :], in_=o_sb[:])
 
-        def is_q(u):
-            return 0 <= u < NU and units[u][0] == 1
-
-        nc.sync.dma_start(out=cos_sb[0][:], in_=cos_t[0:P, :])
+        load_tables(0)
         load(0)
-        nc.sync.dma_start(out=sin_sb[0][:], in_=sin_t[0:P, :])
+        load_tables(1)
         for u in range(1, AHEAD):
             load(u)
         nc.scalar.dma_start(out=v_raw[:], in_=Vf.rearrange("(j p) d -> p j d", p=P))
-        nc.scalar.copy(out=v_grp[:], in_=v_raw[:].rearrange("p j d -> p d j"))
-        nc.vector.quantize_mx(
-            out=vcodes[:].bitcast(FP8X4), scales=vscales[:], in_=v_grp[:].rearrange("p d j -> p (d j)")
-        )
-        idle = scp.tile([P, TT, P], F32, name="sc")
-        negate_sin(0)
-        tables_flip(0)
-        for part in range(3):
-            tables_back(0, part)
+        prepare_sin(0)
 
-        for s in range(NU + 4):
-            if s < NU and units[s][0] == 0 and units[s][2] == 0 and units[s][1] + 1 < TT:
-                load_tables(units[s][1] + 1)
+        for s in range(NU + 5):
+            if s + 2 < TT:
+                load_tables(s + 2)
             if s + AHEAD < NU:
                 load(s + AHEAD)
-            last_of_phase = s < NU - 1 and units[s][2] == H - 1
-            next_tau = units[s + 1][1] if s < NU - 1 else 0
+            groups = []
+            if is_q(s - 2):
+                groups.extend([(s - 2, 0), (s - 2, 1)])
+                if not spread(s - 2):
+                    groups.extend([(s - 2, 2), (s - 2, 3)])
+            if spread(s - 3):
+                groups.extend([(s - 3, 2), (s - 3, 3)])
+            finished = [u for u, tk in groups if tk == TT - 1]
+            ready = [u for u in (s - 3, s - 4) if is_q(u) and u + (4 if spread(u) else 3) == s]
+            renew = s + 1 < NU and not units[s + 1][3] and (units[s][3] or units[s][1] != units[s + 1][1])
             if 0 <= s - 2 < NU:
                 quantise(s - 2)
             if s < NU:
                 products_begin(s)
-                product_sin_gpsimd(s)
-                product_cos(s, 0)
-            if is_q(s - 3):
-                scores_quantise(s - 3)
+                if not units[s][3]:
+                    product(s, 3)
+                product(s, 0)
+            for u in ready:
+                scores_quantise(u)
             if s < NU:
-                product_cos(s, 1)
-                product_sin_vector(s)
-            if s < NU and units[s][0] == 0 and units[s][2] == 2 and units[s][1] + 1 < TT:
-                negate_sin(units[s][1] + 1)
-                tables_flip(units[s][1] + 1)
+                product(s, 1)
+                product(s, 2)
+                if units[s][3]:
+                    product(s, 3)
+            if s == 4:
+                nc.vector.quantize_mx(
+                    out=vcodes[:].bitcast(FP8X4), scales=vscales[:], in_=v_grp[:].rearrange("p d j -> p (d j)")
+                )
+            if s + 1 < TT:
+                prepare_sin(s + 1)
+            if s == 2:
+                nc.scalar.copy(out=v_grp[:], in_=v_raw[:].rearrange("p j d -> p d j"))
+            if s >= 2 and s % 2 == 0 and (s - 2) // 2 < TT:
+                tables_flip((s - 2) // 2)
             if 0 <= s - 1 < NU:
-                rotate_sum(s - 1)
-            if last_of_phase:
-                tables_back(next_tau, 0)
-                tables_back(next_tau, 1)
-            if is_q(s - 2):
-                scores(s - 2)
-            elif 0 <= s - 1 < NU:
-                for k in range(16):
-                    nc.tensor.matmul_mx(
-                        out=idle[:, k % 4, :],
-                        lhsT=vcodes[:, 0:P].bitcast(FP8X4),
-                        lhsT_scale=vscales[:, 0:P],
-                        rhs=vcodes[:, P : 2 * P].bitcast(FP8X4),
-                        rhs_scale=vscales[:, P : 2 * P],
-                        start=True,
-                        stop=True,
-                    )
-            if is_q(s - 3):
-                values(s - 3)
-            if last_of_phase:
-                tables_back(next_tau, 2)
-            if is_q(s - 2):
-                scores_out(s - 2)
-            if is_q(s - 3):
-                store(s - 3)
+                rotate_sum(s - 1, (0, 1))
+            for u, tk in groups[: len(groups) // 2]:
+                scores(u, tk)
+            if 0 <= s - 1 < NU:
+                rotate_sum(s - 1, (2, 3))
+            if renew:
+                tables_back(units[s + 1][1], 0)
+                tables_back(units[s + 1][1], 1)
+            for u, tk in groups[len(groups) // 2 :]:
+                scores(u, tk)
+            for u in ready:
+                values(u)
+            if renew:
+                tables_back(units[s + 1][1], 2)
+            for u in finished:
+                scores_out(u)
+            for u in ready:
+                store(u)

@@ -38,21 +38,14 @@ def tile_bidirectionalattention_pa_kernel(tc, Q, K, V, cos_t, sin_t, out):
     inv_sqrt_n = 1.0 / (float(N) ** 0.5)
 
     units = []
-    for tau in range(TT):
-        units.append((0, tau, 0, True))
-    for h in range(H - 1):
+    for is_query in range(2):
         for tau in range(TT):
-            units.append((1, tau, h, False))
-            units.append((0, tau, h + 1, False))
-    for tau in range(TT):
-        units.append((1, tau, H - 1, True))
+            for h in range(H):
+                units.append((is_query, tau, h, is_query == 0))
     NU = len(units)
 
     def is_q(u):
         return 0 <= u < NU and units[u][0] == 1
-
-    def spread(u):
-        return is_q(u) and u + 1 < NU and units[u + 1][0] == 0
 
     with ExitStack() as ctx:
         const = ctx.enter_context(tc.tile_pool(name="const", bufs=1))
@@ -76,7 +69,7 @@ def tile_bidirectionalattention_pa_kernel(tc, Q, K, V, cos_t, sin_t, out):
         for tau in range(TT):
             cos_sb.append(const.tile([P, N], BF16, name="cos%d" % tau))
             sin_lo.append(const.tile([P, 2 * NB], BF16, name="sinlo%d" % tau))
-            sin_hi.append(const.tile([P, 2, NI - NB], BF16, name="sinhi%d" % tau))
+            sin_hi.append(const.tile([P, 2, NI], BF16, name="sinpl%d" % tau))
             tab_t.append(const.tile([P, NTB, P], F32, name="tabt%d" % tau))
         kcodes = const.tile([P, H * TT, 512], U32, name="kcodes", align_bytes=64)
         kscales = const.tile([P, H * TT, 512], U8, name="kscales", align_bytes=64)
@@ -106,8 +99,8 @@ def tile_bidirectionalattention_pa_kernel(tc, Q, K, V, cos_t, sin_t, out):
             lo = pair_view(sin_lo[tau][:])
             nc.scalar.copy(out=lo[:, 0, :], in_=sv[:, 1, 0:NB])
             nc.scalar.mul(out=lo[:, 1, :], in_=sv[:, 0, 0:NB], mul=-1.0)
-            nc.scalar.copy(out=sin_hi[tau][:, 0, :], in_=sv[:, 1, NB:NI])
-            nc.scalar.mul(out=sin_hi[tau][:, 1, :], in_=sv[:, 0, NB:NI], mul=-1.0)
+            nc.scalar.copy(out=sin_hi[tau][:, 0, :], in_=sv[:, 1, :])
+            nc.scalar.mul(out=sin_hi[tau][:, 1, :], in_=sv[:, 0, :], mul=-1.0)
 
         def tables_flip(tau):
             cw = cos_sb[tau][:].bitcast(F32)
@@ -131,23 +124,26 @@ def tile_bidirectionalattention_pa_kernel(tc, Q, K, V, cos_t, sin_t, out):
             b = prod.tile([P, 2, NI], F32, name="b")
             state[("ab", u)] = (a, b)
 
+        def product_alone(u, sine):
+            tau = units[u][1]
+            xv = pair_view(state[("x", u)][:])
+            a, b = state[("ab", u)]
+            if sine:
+                nc.vector.tensor_tensor(out=b[:], in0=xv, in1=sin_hi[tau][:], op=MULT)
+            else:
+                nc.vector.tensor_tensor(out=a[:], in0=xv, in1=pair_view(cos_sb[tau][:]), op=MULT)
+
         def product(u, part):
-            is_query, tau, h, alone = units[u]
+            tau = units[u][1]
             xv = pair_view(state[("x", u)][:])
             a, b = state[("ab", u)]
             rng = slice((part % 2) * 512, (part % 2) * 512 + 512)
             dst = a if part < 2 else b
             if part == 3:
-                eng = nc.vector if alone else nc.gpsimd
-                eng.tensor_tensor(out=dst[:, :, rng], in0=xv[:, :, rng], in1=sin_hi[tau][:], op=MULT)
-                return
-            if not alone:
-                tab = pair_view(state[("tab", part)][:].bitcast(BF16))
-            elif part == 2:
-                tab = pair_view(sin_lo[tau][:])
+                nc.gpsimd.tensor_tensor(out=dst[:, :, rng], in0=xv[:, :, rng], in1=sin_hi[tau][:, :, rng], op=MULT)
             else:
-                tab = pair_view(cos_sb[tau][:])[:, :, rng]
-            nc.vector.tensor_tensor(out=dst[:, :, rng], in0=xv[:, :, rng], in1=tab, op=MULT)
+                tab = pair_view(state[("tab", part)][:].bitcast(BF16))
+                nc.vector.tensor_tensor(out=dst[:, :, rng], in0=xv[:, :, rng], in1=tab, op=MULT)
 
         def rotate_sum(u, banks):
             a, b = state[("ab", u)]
@@ -238,68 +234,58 @@ def tile_bidirectionalattention_pa_kernel(tc, Q, K, V, cos_t, sin_t, out):
             nc.sync.dma_start(out=outf[r0 : r0 + P, :], in_=o_sb[:])
 
         load_tables(0)
-        load(0)
-        load_tables(1)
-        for u in range(1, AHEAD):
+        for u in range(AHEAD):
             load(u)
         nc.scalar.dma_start(out=v_raw[:], in_=Vf.rearrange("(j p) d -> p j d", p=P))
         prepare_sin(0)
 
-        for s in range(NU + 5):
-            if s + 2 < TT:
-                load_tables(s + 2)
+        for s in range(NU + 4):
+            is_query, tau, h, alone = units[min(s, NU - 1)]
+            if s < NU and alone and h == 0 and tau + 1 < TT:
+                load_tables(tau + 1)
             if s + AHEAD < NU:
                 load(s + AHEAD)
-            groups = []
-            if is_q(s - 2):
-                groups.extend([(s - 2, 0), (s - 2, 1)])
-                if not spread(s - 2):
-                    groups.extend([(s - 2, 2), (s - 2, 3)])
-            if spread(s - 3):
-                groups.extend([(s - 3, 2), (s - 3, 3)])
-            finished = [u for u, tk in groups if tk == TT - 1]
-            ready = [u for u in (s - 3, s - 4) if is_q(u) and u + (4 if spread(u) else 3) == s]
-            renew = s + 1 < NU and not units[s + 1][3] and (units[s][3] or units[s][1] != units[s + 1][1])
+            renew = s + 1 < NU and not units[s + 1][3] and (alone or tau != units[s + 1][1])
             if 0 <= s - 2 < NU:
                 quantise(s - 2)
             if s < NU:
                 products_begin(s)
-                if not units[s][3]:
+                if alone:
+                    product_alone(s, False)
+                else:
                     product(s, 3)
-                product(s, 0)
-            for u in ready:
-                scores_quantise(u)
+                    product(s, 0)
+            if is_q(s - 3):
+                scores_quantise(s - 3)
             if s < NU:
-                product(s, 1)
-                product(s, 2)
-                if units[s][3]:
-                    product(s, 3)
+                if alone:
+                    product_alone(s, True)
+                else:
+                    product(s, 1)
+                    product(s, 2)
             if s == 4:
                 nc.vector.quantize_mx(
                     out=vcodes[:].bitcast(FP8X4), scales=vscales[:], in_=v_grp[:].rearrange("p d j -> p (d j)")
                 )
-            if s + 1 < TT:
-                prepare_sin(s + 1)
+            if s < NU and alone and h == 1 and tau + 1 < TT:
+                prepare_sin(tau + 1)
             if s == 2:
                 nc.scalar.copy(out=v_grp[:], in_=v_raw[:].rearrange("p j d -> p d j"))
-            if s >= 2 and s % 2 == 0 and (s - 2) // 2 < TT:
-                tables_flip((s - 2) // 2)
+            if s < NU and alone and h == 2:
+                tables_flip(tau)
             if 0 <= s - 1 < NU:
-                rotate_sum(s - 1, (0, 1))
-            for u, tk in groups[: len(groups) // 2]:
-                scores(u, tk)
-            if 0 <= s - 1 < NU:
-                rotate_sum(s - 1, (2, 3))
+                rotate_sum(s - 1, (0, 1, 2, 3))
             if renew:
                 tables_back(units[s + 1][1], 0)
                 tables_back(units[s + 1][1], 1)
-            for u, tk in groups[len(groups) // 2 :]:
-                scores(u, tk)
-            for u in ready:
-                values(u)
+            if is_q(s - 2):
+                for tk in range(TT):
+                    scores(s - 2, tk)
+            if is_q(s - 3):
+                values(s - 3)
             if renew:
                 tables_back(units[s + 1][1], 2)
-            for u in finished:
-                scores_out(u)
-            for u in ready:
-                store(u)
+            if is_q(s - 2):
+                scores_out(s - 2)
+            if is_q(s - 3):
+                store(s - 3)

from contextlib import ExitStack

import concourse.mybir as mybir
from concourse.masks import make_identity

F32 = mybir.dt.float32
BF16 = mybir.dt.bfloat16
U32 = mybir.dt.uint32
U8 = mybir.dt.uint8
FP8X4 = mybir.dt.float8_e4m3fn_x4
MULT = mybir.AluOpType.mult
COPY = mybir.ActivationFunctionType.Copy

P = 128
H = 4
T = 512
N = 2048
D = 256
TT = T // P
NG = N // 512
NI = N // 2
NB = 512
NTB = 8 + NB // P
AHEAD = 3
FLOPS = 2 * H * T * T * N + 2 * H * T * T * D


def pair_view(ap):
    return ap.rearrange("p (i e) -> p e i", e=2)


def tile_bidirectionalattention_pa_kernel(tc, Q, K, V, cos_t, sin_t, out):
    nc = tc.nc
    Qf = Q.flatten_outer_dims()
    Kf = K.flatten_outer_dims()
    Vf = V.flatten_outer_dims()
    outf = out.flatten_outer_dims()
    inv_sqrt_n = 1.0 / (float(N) ** 0.5)

    units = []
    for is_query in range(2):
        for tau in range(TT):
            for h in range(H):
                units.append((is_query, tau, h, is_query == 0))
    NU = len(units)

    def is_q(u):
        return 0 <= u < NU and units[u][0] == 1

    with ExitStack() as ctx:
        const = ctx.enter_context(tc.tile_pool(name="const", bufs=1))
        rawp = ctx.enter_context(tc.tile_pool(name="rawp", bufs=2))
        xpool = ctx.enter_context(tc.tile_pool(name="xpool", bufs=AHEAD + 1))
        prod = ctx.enter_context(tc.tile_pool(name="prod", bufs=3))
        gpool = ctx.enter_context(tc.tile_pool(name="gpool", bufs=3))
        qpool = ctx.enter_context(tc.tile_pool(name="qpool", bufs=2))
        spool = ctx.enter_context(tc.tile_pool(name="spool", bufs=2))
        tabp = ctx.enter_context(tc.psum_pool(name="tabp", bufs=1))
        accp = ctx.enter_context(tc.psum_pool(name="accp", bufs=4))
        scp = ctx.enter_context(tc.psum_pool(name="scp", bufs=1))
        ctx.enter_context(tc.manual_schedule())

        ident = const.tile([P, P], F32, name="ident")
        make_identity(nc, ident[:])
        cos_sb = []
        sin_lo = []
        sin_hi = []
        tab_t = []
        for tau in range(TT):
            cos_sb.append(const.tile([P, N], BF16, name="cos%d" % tau))
            sin_lo.append(const.tile([P, 2 * NB], BF16, name="sinlo%d" % tau))
            sin_hi.append(const.tile([P, 2, NI], BF16, name="sinpl%d" % tau))
            tab_t.append(const.tile([P, NTB, P], F32, name="tabt%d" % tau))
        kcodes = const.tile([P, H * TT, 512], U32, name="kcodes", align_bytes=64)
        kscales = const.tile([P, H * TT, 512], U8, name="kscales", align_bytes=64)
        v_raw = const.tile([P, 4, D], BF16, name="v_raw")
        v_grp = const.tile([P, D, 4], BF16, name="v_grp", align_bytes=64)
        vcodes = const.tile([P, D], U32, name="vcodes", align_bytes=64)
        vscales = const.tile([P, D], U8, name="vscales", align_bytes=64)
        state = {}

        def load_tables(tau):
            rows = slice(tau * P, (tau + 1) * P)
            nc.sync.dma_start(out=cos_sb[tau][:], in_=cos_t[rows, :])
            raw = rawp.tile([P, N], BF16, name="sinraw")
            nc.sync.dma_start(out=raw[:], in_=sin_t[rows, :])
            state[("sinraw", tau)] = raw

        def load(u):
            is_query, tau, h, alone = units[u]
            src = Qf if is_query else Kf
            x = xpool.tile([P, N], BF16, name="x")
            r0 = h * T + tau * P
            nc.sync.dma_start(out=x[:], in_=src[r0 : r0 + P, :])
            state[("x", u)] = x

        def prepare_sin(tau):
            sv = pair_view(state[("sinraw", tau)][:])
            lo = pair_view(sin_lo[tau][:])
            nc.scalar.copy(out=lo[:, 0, :], in_=sv[:, 1, 0:NB])
            nc.scalar.mul(out=lo[:, 1, :], in_=sv[:, 0, 0:NB], mul=-1.0)
            nc.scalar.copy(out=sin_hi[tau][:, 0, :], in_=sv[:, 1, :])
            nc.scalar.mul(out=sin_hi[tau][:, 1, :], in_=sv[:, 0, :], mul=-1.0)

        def tables_flip(tau):
            cw = cos_sb[tau][:].bitcast(F32)
            sw = sin_lo[tau][:].bitcast(F32)
            for b0 in range(0, NTB, 4):
                ps = accp.tile([P, 4, P], F32, name="ps")
                for k in range(4):
                    b = b0 + k
                    srcw = cw[:, b * P : (b + 1) * P] if b < 8 else sw[:, (b - 8) * P : (b - 7) * P]
                    nc.tensor.transpose(ps[:, k, :], srcw, ident[:])
                nc.scalar.copy(out=tab_t[tau][:, b0 : b0 + 4, :], in_=ps[:])

        def tables_back(tau, part):
            t = tabp.tile([P, 512], F32, name="tab%d" % part)
            for k in range(4):
                nc.tensor.transpose(t[:, k * P : (k + 1) * P], tab_t[tau][:, 4 * part + k, :], ident[:])
            state[("tab", part)] = t

        def products_begin(u):
            a = prod.tile([P, 2, NI], F32, name="a")
            b = prod.tile([P, 2, NI], F32, name="b")
            state[("ab", u)] = (a, b)

        def product_alone(u, sine):
            tau = units[u][1]
            xv = pair_view(state[("x", u)][:])
            a, b = state[("ab", u)]
            if sine:
                nc.vector.tensor_tensor(out=b[:], in0=xv, in1=sin_hi[tau][:], op=MULT)
            else:
                nc.vector.tensor_tensor(out=a[:], in0=xv, in1=pair_view(cos_sb[tau][:]), op=MULT)

        def product(u, part):
            tau = units[u][1]
            xv = pair_view(state[("x", u)][:])
            a, b = state[("ab", u)]
            rng = slice((part % 2) * 512, (part % 2) * 512 + 512)
            dst = a if part < 2 else b
            if part == 3:
                nc.gpsimd.tensor_tensor(out=dst[:, :, rng], in0=xv[:, :, rng], in1=sin_hi[tau][:, :, rng], op=MULT)
            else:
                tab = pair_view(state[("tab", part)][:].bitcast(BF16))
                nc.vector.tensor_tensor(out=dst[:, :, rng], in0=xv[:, :, rng], in1=tab, op=MULT)

        def rotate_sum(u, banks):
            a, b = state[("ab", u)]
            if banks[0] == 0:
                state[("grp", u)] = gpool.tile([P, NG, P, 4], BF16, name="grp", align_bytes=64)
            grp = state[("grp", u)]
            for g in banks:
                ps = accp.tile([P, 4, P], F32, name="ps")
                for j in range(4):
                    e = j % 2
                    c = 2 * g + j // 2
                    cols = slice(c * P, (c + 1) * P)
                    nc.tensor.matmul(
                        out=ps[:, j, :], lhsT=a[:, e, cols], rhs=ident[:], start=True, stop=False, is_transpose=True
                    )
                    nc.tensor.matmul(
                        out=ps[:, j, :], lhsT=b[:, 1 - e, cols], rhs=ident[:], start=False, stop=True, is_transpose=True
                    )
                nc.scalar.copy(out=grp[:, g, :, :], in_=ps[:].rearrange("p j t -> p t j"))

        def quantise(u):
            is_query, tau, h, alone = units[u]
            grp = state[("grp", u)]
            if is_query:
                qc = qpool.tile([P, 512], U32, name="qc", align_bytes=64)
                qs = qpool.tile([P, 512], U8, name="qs", align_bytes=64)
                codes = qc[:]
                scales = qs[:]
                state[("q", u)] = (qc, qs)
            else:
                codes = kcodes[:, h * TT + tau, :]
                scales = kscales[:, h * TT + tau, :]
            nc.vector.quantize_mx(
                out=codes.bitcast(FP8X4), scales=scales, in_=grp[:].rearrange("p g t j -> p (g t j)")
            )

        def scores(u, tk):
            h = units[u][2]
            qc, qs = state[("q", u)]
            if tk == 0:
                state[("sc", u)] = scp.tile([P, TT, P], F32, name="sc")
            sc = state[("sc", u)]
            for g in range(NG):
                cols = slice(g * P, (g + 1) * P)
                nc.tensor.matmul_mx(
                    out=sc[:, tk, :],
                    lhsT=kcodes[:, h * TT + tk, cols].bitcast(FP8X4),
                    lhsT_scale=kscales[:, h * TT + tk, cols],
                    rhs=qc[:, cols].bitcast(FP8X4),
                    rhs_scale=qs[:, cols],
                    start=(g == 0),
                    stop=(g == NG - 1),
                )

        def scores_out(u):
            sc = state[("sc", u)]
            sg = spool.tile([P, P, 4], BF16, name="sg", align_bytes=64)
            nc.scalar.activation(out=sg[:], in_=sc[:].rearrange("p j q -> p q j"), func=COPY, scale=inv_sqrt_n)
            state[("sg", u)] = sg

        def scores_quantise(u):
            sg = state[("sg", u)]
            scd = spool.tile([P, P], U32, name="scd", align_bytes=64)
            ssc = spool.tile([P, P], U8, name="ssc", align_bytes=64)
            nc.vector.quantize_mx(out=scd[:].bitcast(FP8X4), scales=ssc[:], in_=sg[:].rearrange("p q j -> p (q j)"))
            state[("scd", u)] = (scd, ssc)

        def values(u):
            scd, ssc = state[("scd", u)]
            ps = accp.tile([P, 4, P], F32, name="ps")
            o_ps = ps[:].rearrange("p j t -> p (j t)")[:, 0:D]
            nc.tensor.matmul_mx(
                out=o_ps,
                lhsT=scd[:].bitcast(FP8X4),
                lhsT_scale=ssc[:],
                rhs=vcodes[:].bitcast(FP8X4),
                rhs_scale=vscales[:],
                start=True,
                stop=True,
            )
            state[("o", u)] = o_ps

        def store(u):
            is_query, tau, h, alone = units[u]
            o_sb = spool.tile([P, D], F32, name="o_sb")
            nc.scalar.copy(out=o_sb[:], in_=state[("o", u)])
            r0 = h * T + tau * P
            nc.sync.dma_start(out=outf[r0 : r0 + P, :], in_=o_sb[:])

        load_tables(0)
        for u in range(AHEAD):
            load(u)
        nc.scalar.dma_start(out=v_raw[:], in_=Vf.rearrange("(j p) d -> p j d", p=P))
        prepare_sin(0)

        for s in range(NU + 4):
            is_query, tau, h, alone = units[min(s, NU - 1)]
            if s < NU and alone and h == 0 and tau + 1 < TT:
                load_tables(tau + 1)
            if s + AHEAD < NU:
                load(s + AHEAD)
            renew = s + 1 < NU and not units[s + 1][3] and (alone or tau != units[s + 1][1])
            if 0 <= s - 2 < NU:
                quantise(s - 2)
            if s < NU:
                products_begin(s)
                if alone:
                    product_alone(s, False)
                else:
                    product(s, 3)
                    product(s, 0)
            if is_q(s - 3):
                scores_quantise(s - 3)
            if s < NU:
                if alone:
                    product_alone(s, True)
                else:
                    product(s, 1)
                    product(s, 2)
            if s == 4:
                nc.vector.quantize_mx(
                    out=vcodes[:].bitcast(FP8X4), scales=vscales[:], in_=v_grp[:].rearrange("p d j -> p (d j)")
                )
            if s < NU and alone and h == 1 and tau + 1 < TT:
                prepare_sin(tau + 1)
            if s == 2:
                nc.scalar.copy(out=v_grp[:], in_=v_raw[:].rearrange("p j d -> p d j"))
            if s < NU and alone and h == 2:
                tables_flip(tau)
            if 0 <= s - 1 < NU:
                rotate_sum(s - 1, (0, 1, 2, 3))
            if renew:
                tables_back(units[s + 1][1], 0)
                tables_back(units[s + 1][1], 1)
            if is_q(s - 2):
                for tk in range(TT):
                    scores(s - 2, tk)
            if is_q(s - 3):
                values(s - 3)
            if renew:
                tables_back(units[s + 1][1], 2)
            if is_q(s - 2):
                scores_out(s - 2)
            if is_q(s - 3):
                store(s - 3)
